import numpy as np
import ml_dtypes


def mxq(x, axis, fmt="e4m3"):
    dtype, down = {"e4m3": (ml_dtypes.float8_e4m3fn, 7), "e5m2": (ml_dtypes.float8_e5m2, 14)}[fmt]
    v = np.moveaxis(np.asarray(x, np.float32).astype(ml_dtypes.bfloat16).astype(np.float64), axis, -1)
    blocks = v.reshape(v.shape[:-1] + (-1, 32))
    amax = np.abs(blocks).max(-1, keepdims=True)
    byte = np.maximum(np.where(amax > 0, np.frexp(amax)[1] - 1 + 127, 0) - down, 1)
    scale = np.exp2(byte - 127.0)
    codes = (blocks / scale).astype(np.float32).astype(dtype).astype(np.float64)
    return np.moveaxis((codes * scale).reshape(v.shape), -1, axis)


WIDE = False


def mx_kscale(k):
    if not WIDE:
        return np.ones(k)
    levels = np.array([10, -10, 5, -5, 0])
    a = np.random.permutation(np.resize(levels, k // 512 * 4)).reshape(k // 512, 4)
    idx = np.arange(k)
    return np.exp2(a[idx // 512, idx % 128 // 32])


BF16 = ml_dtypes.bfloat16


def bf(x):
    return np.asarray(x, np.float32).astype(BF16)


def f64(x):
    return np.asarray(x).astype(np.float64)


B, L, D, H, QK, V = 4, 512, 1024, 8, 128, 128


def setup_inputs():
    s = mx_kscale(L)
    return {"q_rot": bf(np.random.standard_normal((H, B, L, QK)) * 0.3),
            "k_rot": bf(np.random.standard_normal((H, B, L, QK)) * 0.3 * s[:, None]),
            "v": bf(np.random.standard_normal((H, B, L, V)) * 0.5 / s[:, None]),
            "times": bf(np.broadcast_to(np.arange(L), (B, L)))}


def reference(q_rot, k_rot, v, times):
    gammas = 1.0 - 2.0 ** (-5.0 - np.arange(H))
    t = f64(times)
    mat = t[:, :, None] - t[:, None, :]
    mask = mat >= 0
    g4 = gammas[:, None, None, None]
    d = np.where(mask, g4 ** np.where(mask, mat, 0.0), 0.0)
    ret = (f64(q_rot) @ f64(k_rot).transpose(0, 1, 3, 2)) * d
    return mxq(ret, 3, "e4m3") @ mxq(f64(v), 2, "e4m3")

@@ -1,0 +1,218 @@
+import math
+from contextlib import ExitStack
+
+import concourse.mybir as mybir
+from concourse.masks import make_identity
+
+F32 = mybir.dt.float32
+BF16 = mybir.dt.bfloat16
+U32 = mybir.dt.uint32
+U8 = mybir.dt.uint8
+FP8X4 = mybir.dt.float8_e4m3fn_x4
+ALU = mybir.AluOpType
+ACT = mybir.ActivationFunctionType
+
+H, B, L, DH = 8, 4, 512, 128
+P = 128
+NT = L // P
+STEPS = H * B
+PAIR = 2
+FAR = 1.0e6
+LOG_GAMMA = [math.log(1.0 - 2.0 ** (-5 - h)) for h in range(H)]
+
+FLOPS = 2 * (2 * H * B * L * L * DH)
+
+
+def tile_multiscaleretention_pb_kernel(tc, q_rot, k_rot, v, times, out):
+    nc = tc.nc
+    q_rows = q_rot.flatten_outer_dims().rearrange("(g p) d -> p g d", p=P)
+    k_rows = k_rot.flatten_outer_dims().rearrange("(g p) d -> p g d", p=P)
+    v_rows = v.flatten_outer_dims().rearrange("(g p) d -> p g d", p=P)
+    out_rows = out.flatten_outer_dims().rearrange("(g p) d -> p g d", p=P)
+
+    with ExitStack() as stack:
+        stack.enter_context(tc.manual_schedule())
+        const = stack.enter_context(tc.tile_pool(name="const", bufs=1))
+        small = stack.enter_context(tc.tile_pool(name="small", bufs=2))
+        loads = stack.enter_context(tc.tile_pool(name="loads", bufs=3))
+        turned = stack.enter_context(tc.tile_pool(name="turned", bufs=3))
+        weighed = stack.enter_context(tc.tile_pool(name="weighed", bufs=2))
+        values = stack.enter_context(tc.tile_pool(name="values", bufs=3))
+        results = stack.enter_context(tc.tile_pool(name="results", bufs=3))
+        turn_psum = stack.enter_context(tc.psum_pool(name="turn_psum", bufs=2))
+        score_psum = stack.enter_context(tc.psum_pool(name="score_psum", bufs=NT))
+        out_psum = stack.enter_context(tc.psum_pool(name="out_psum", bufs=2))
+
+        q_sb, k_sb, v_sb = {}, {}, {}
+        v_codes, v_scales, v_grouped = {}, {}, {}
+        qk_t, scores, ret_bf, ret_codes, ret_scales = {}, {}, {}, {}, {}
+
+        def load(c):
+            slots = slice(c * PAIR * NT, (c + 1) * PAIR * NT)
+            q_sb[c] = loads.tile([P, PAIR * NT, DH], BF16, name="q_sb")
+            k_sb[c] = loads.tile([P, PAIR * NT, DH], BF16, name="k_sb")
+            v_sb[c] = loads.tile([P, PAIR, NT, DH], BF16, name="v_sb")
+            nc.sync.dma_start(out=q_sb[c][:], in_=q_rows[:, slots, :])
+            nc.sync.dma_start(out=k_sb[c][:], in_=k_rows[:, slots, :])
+            nc.sync.dma_start(
+                out=v_sb[c][:].rearrange("p b t d -> p (b t) d"), in_=v_rows[:, slots, :]
+            )
+
+        def regroup_v(c):
+            v_grouped[c] = values.tile([P, PAIR, DH, NT], BF16, name="v_grouped", align_bytes=64)
+            nc.scalar.copy(out=v_grouped[c][:], in_=v_sb[c][:].rearrange("p b t d -> p b d t"))
+
+        def quantise_v(c):
+            v_codes[c] = values.tile([P, PAIR, DH], U32, name="v_codes", align_bytes=64)
+            v_scales[c] = values.tile([P, PAIR, DH], U8, name="v_scales", align_bytes=64)
+            nc.vector.quantize_mx(
+                out=v_codes[c][:].rearrange("p b d -> p (b d)").bitcast(FP8X4),
+                scales=v_scales[c][:].rearrange("p b d -> p (b d)"),
+                in_=v_grouped[c][:].rearrange("p b d t -> p (b d t)"),
+            )
+
+        def turn(n):
+            c, first = n // PAIR, (n % PAIR) * NT
+            bank = turn_psum.tile([P, 2 * NT, P], BF16, name="turn_bank")
+            for a in range(NT):
+                nc.tensor.transpose(out=bank[:, a, :], in_=q_sb[c][:, first + a, :], identity=ident[:])
+            for a in range(NT):
+                nc.tensor.transpose(
+                    out=bank[:, NT + a, :], in_=k_sb[c][:, first + a, :], identity=ident[:]
+                )
+            qk_t[n] = turned.tile([P, 2 * NT, P], BF16, name="qk_t")
+            nc.scalar.copy(out=qk_t[n][:], in_=bank[:])
+
+        def decay_of(n):
+            h, b = divmod(n, B)
+            for i_tile in range(NT):
+                nc.scalar.activation(
+                    out=decay[b][:, i_tile, 0 : i_tile + 1, :],
+                    in_=delta[b][:, i_tile, 0 : i_tile + 1, :],
+                    func=ACT.Exp,
+                    scale=LOG_GAMMA[h],
+                )
+
+        def score(n, i_tile):
+            scores[n, i_tile] = score_psum.tile([P, NT, P], F32, name="score_bank")
+            for t in range(NT):
+                nc.tensor.matmul(
+                    out=scores[n, i_tile][:, t, :],
+                    lhsT=qk_t[n][:, NT + t, :],
+                    rhs=qk_t[n][:, i_tile, :],
+                    start=True,
+                    stop=True,
+                )
+
+        def weigh(n, i_tile):
+            b = n % B
+            if i_tile == 0:
+                ret_bf[n] = weighed.tile([P, NT, P, NT], BF16, name="ret_bf", align_bytes=64)
+            nc.vector.tensor_tensor(
+                out=ret_bf[n][:, i_tile, :, :],
+                in0=scores[n, i_tile][:].rearrange("p t i -> p i t"),
+                in1=decay[b][:, i_tile, :, :].rearrange("p t i -> p i t"),
+                op=ALU.mult,
+            )
+
+        def quantise(n):
+            ret_codes[n] = weighed.tile([P, L], U32, name="ret_codes", align_bytes=64)
+            ret_scales[n] = weighed.tile([P, L], U8, name="ret_scales", align_bytes=64)
+            nc.vector.quantize_mx(
+                out=ret_codes[n][:].bitcast(FP8X4),
+                scales=ret_scales[n][:],
+                in_=ret_bf[n][:].rearrange("p a i t -> p (a i t)"),
+            )
+
+        def product(n):
+            c, half = n // PAIR, n % PAIR
+            bank = out_psum.tile([P, NT, DH], F32, name="out_bank")
+            for i_tile in range(NT):
+                cols = slice(i_tile * P, (i_tile + 1) * P)
+                nc.tensor.matmul_mx(
+                    out=bank[:, i_tile, :],
+                    lhsT=ret_codes[n][:, cols].bitcast(FP8X4),
+                    lhsT_scale=ret_scales[n][:, cols],
+                    rhs=v_codes[c][:, half, :].bitcast(FP8X4),
+                    rhs_scale=v_scales[c][:, half, :],
+                    start=True,
+                    stop=True,
+                )
+            out_sb = results.tile([P, NT, DH], F32, name="out_sb")
+            nc.scalar.copy(out=out_sb[:], in_=bank[:])
+            nc.sync.dma_start(out=out_rows[:, n * NT : (n + 1) * NT, :], in_=out_sb[:])
+
+        t_row = const.tile([P, B * L], BF16, name="t_row")
+        t_src = const.tile([P, P], BF16, name="t_src")
+        nc.vector.memset(t_src[:], 0.0)
+        nc.scalar.dma_start(out=t_src[0 : B * NT, :], in_=times.rearrange("b (t p) -> (b t) p", p=P))
+        nc.scalar.dma_start(out=t_row[:], in_=times.rearrange("b l -> (b l)").partition_broadcast(P))
+        load(0)
+        load(1)
+        ident = const.tile([P, P], BF16, name="ident")
+        make_identity(nc, ident[:])
+
+        t_bank = turn_psum.tile([P, 2 * NT, P], BF16, name="turn_bank")
+        nc.tensor.transpose(out=t_bank[:, 0, :], in_=t_src[:], identity=ident[:])
+        t_key = const.tile([P, B * NT], F32, name="t_key")
+        minus_t_key = const.tile([P, B * NT], F32, name="minus_t_key")
+        nc.vector.tensor_copy(out=t_key[:], in_=t_bank[:, 0, 0 : B * NT])
+        nc.vector.tensor_scalar_mul(out=minus_t_key[:], in0=t_key[:], scalar1=-1.0)
+
+        delta = [const.tile([P, NT, NT, P], F32, name="delta%d" % b) for b in range(B)]
+        decay = [const.tile([P, NT, NT, P], F32, name="decay%d" % b) for b in range(B)]
+
+        def prepare_times(b):
+            row = t_row[:, b * L : (b + 1) * L].rearrange("p (a i) -> p a i", i=P)
+            for t in range(NT):
+                key_time = t_key[:, b * NT + t : b * NT + t + 1]
+                dead = small.tile([P, P], F32, name="dead")
+                nc.vector.tensor_scalar(
+                    out=dead[:], in0=row[:, t, :], scalar1=key_time, scalar2=FAR,
+                    op0=ALU.is_lt, op1=ALU.mult,
+                )
+                nc.vector.scalar_tensor_tensor(
+                    out=delta[b][:, t, t, :], in0=row[:, t, :], scalar=key_time, in1=dead[:],
+                    op0=ALU.subtract, op1=ALU.max,
+                )
+                if t + 1 < NT:
+                    nc.scalar.activation(
+                        out=delta[b][:, t + 1 : NT, t, :], in_=row[:, t + 1 : NT, :],
+                        func=ACT.Identity, bias=minus_t_key[:, b * NT + t : b * NT + t + 1], scale=1.0,
+                    )
+                if t > 0:
+                    nc.vector.tensor_scalar(
+                        out=decay[b][:, 0:t, t, :], in0=row[:, 0:t, :], scalar1=key_time, scalar2=None,
+                        op0=ALU.is_ge,
+                    )
+
+        turn(0)
+        prepare_times(0)
+        decay_of(0)
+        for i_tile in range(NT):
+            score(0, i_tile)
+        turn(1)
+        prepare_times(1)
+        decay_of(1)
+        regroup_v(0)
+        prepare_times(2)
+        prepare_times(3)
+        quantise_v(0)
+        for s in range(STEPS + 1):
+            if s % PAIR == 0 and s // PAIR + 2 < STEPS // PAIR:
+                load(s // PAIR + 2)
+            if s + 2 < STEPS:
+                decay_of(s + 2)
+                turn(s + 2)
+            for i_tile in range(NT):
+                if s < STEPS:
+                    weigh(s, i_tile)
+                if s + 1 < STEPS:
+                    score(s + 1, i_tile)
+                if i_tile == 0 and s >= 1:
+                    quantise(s - 1)
+                    product(s - 1)
+            if s % PAIR == 0 and s // PAIR + 1 < STEPS // PAIR:
+                regroup_v(s // PAIR + 1)
+            if s % PAIR == 1 and s // PAIR + 1 < STEPS // PAIR:
+                quantise_v(s // PAIR + 1)

@@ -60,7 +60,15 @@ def tile_multiscaleretention_pb_kernel(tc, q_rot, k_rot, v, times, out):
 
         def regroup_v(c):
             v_grouped[c] = values.tile([P, PAIR, DH, NT], BF16, name="v_grouped", align_bytes=64)
-            nc.scalar.copy(out=v_grouped[c][:], in_=v_sb[c][:].rearrange("p b t d -> p b d t"))
+            for half in range(PAIR):
+                nc.gpsimd.tensor_scalar(
+                    out=v_grouped[c][:, half, :, :],
+                    in0=v_sb[c][:, half, :, :].rearrange("p t d -> p d t"),
+                    scalar1=1.0,
+                    scalar2=0.0,
+                    op0=ALU.mult,
+                    op1=ALU.add,
+                )
 
         def quantise_v(c):
             v_codes[c] = values.tile([P, PAIR, DH], U32, name="v_codes", align_bytes=64)
@@ -146,7 +154,11 @@ def tile_multiscaleretention_pb_kernel(tc, q_rot, k_rot, v, times, out):
         t_src = const.tile([P, P], BF16, name="t_src")
         nc.vector.memset(t_src[:], 0.0)
         nc.scalar.dma_start(out=t_src[0 : B * NT, :], in_=times.rearrange("b (t p) -> (b t) p", p=P))
-        nc.scalar.dma_start(out=t_row[:], in_=times.rearrange("b l -> (b l)").partition_broadcast(P))
+        t_flat = const.tile([P, B * L], BF16, name="t_flat")
+        ones = const.tile([P, P], BF16, name="ones")
+        nc.vector.memset(t_flat[:], 0.0)
+        nc.vector.memset(ones[:], 1.0)
+        nc.scalar.dma_start(out=t_flat[0:1, :], in_=times.rearrange("(o b) l -> o (b l)", o=1))
         load(0)
         load(1)
         ident = const.tile([P, P], BF16, name="ident")
@@ -158,6 +170,18 @@ def tile_multiscaleretention_pb_kernel(tc, q_rot, k_rot, v, times, out):
         minus_t_key = const.tile([P, B * NT], F32, name="minus_t_key")
         nc.vector.tensor_copy(out=t_key[:], in_=t_bank[:, 0, 0 : B * NT])
         nc.vector.tensor_scalar_mul(out=minus_t_key[:], in0=t_key[:], scalar1=-1.0)
+        for b in range(B):
+            row_bank = score_psum.tile([P, NT, P], F32, name="score_bank")
+            nc.tensor.matmul(
+                out=row_bank[:].rearrange("p a i -> p (a i)"),
+                lhsT=ones[:],
+                rhs=t_flat[:, b * L : (b + 1) * L],
+                start=True,
+                stop=True,
+            )
+            nc.scalar.copy(
+                out=t_row[:, b * L : (b + 1) * L], in_=row_bank[:].rearrange("p a i -> p (a i)")
+            )
 
         delta = [const.tile([P, NT, NT, P], F32, name="delta%d" % b) for b in range(B)]
         decay = [const.tile([P, NT, NT, P], F32, name="decay%d" % b) for b in range(B)]
@@ -195,12 +219,12 @@ def tile_multiscaleretention_pb_kernel(tc, q_rot, k_rot, v, times, out):
         prepare_times(1)
         decay_of(1)
         regroup_v(0)
-        prepare_times(2)
-        prepare_times(3)
         quantise_v(0)
         for s in range(STEPS + 1):
             if s % PAIR == 0 and s // PAIR + 2 < STEPS // PAIR:
                 load(s // PAIR + 2)
+            if s + 2 < B:
+                prepare_times(s + 2)
             if s + 2 < STEPS:
                 decay_of(s + 2)
                 turn(s + 2)

@@ -17,6 +17,8 @@ P = 128
 NT = L // P
 STEPS = H * B
 PAIR = 2
+LOADS = STEPS // PAIR
+AHEAD = 5
 FAR = 1.0e6
 LOG_GAMMA = [math.log(1.0 - 2.0 ** (-5 - h)) for h in range(H)]
 
@@ -34,7 +36,7 @@ def tile_multiscaleretention_pb_kernel(tc, q_rot, k_rot, v, times, out):
         stack.enter_context(tc.manual_schedule())
         const = stack.enter_context(tc.tile_pool(name="const", bufs=1))
         small = stack.enter_context(tc.tile_pool(name="small", bufs=2))
-        loads = stack.enter_context(tc.tile_pool(name="loads", bufs=3))
+        loads = stack.enter_context(tc.tile_pool(name="loads", bufs=AHEAD + 1))
         turned = stack.enter_context(tc.tile_pool(name="turned", bufs=3))
         weighed = stack.enter_context(tc.tile_pool(name="weighed", bufs=2))
         values = stack.enter_context(tc.tile_pool(name="values", bufs=3))
@@ -60,15 +62,7 @@ def tile_multiscaleretention_pb_kernel(tc, q_rot, k_rot, v, times, out):
 
         def regroup_v(c):
             v_grouped[c] = values.tile([P, PAIR, DH, NT], BF16, name="v_grouped", align_bytes=64)
-            for half in range(PAIR):
-                nc.gpsimd.tensor_scalar(
-                    out=v_grouped[c][:, half, :, :],
-                    in0=v_sb[c][:, half, :, :].rearrange("p t d -> p d t"),
-                    scalar1=1.0,
-                    scalar2=0.0,
-                    op0=ALU.mult,
-                    op1=ALU.add,
-                )
+            nc.scalar.copy(out=v_grouped[c][:], in_=v_sb[c][:].rearrange("p b t d -> p b d t"))
 
         def quantise_v(c):
             v_codes[c] = values.tile([P, PAIR, DH], U32, name="v_codes", align_bytes=64)
@@ -148,7 +142,7 @@ def tile_multiscaleretention_pb_kernel(tc, q_rot, k_rot, v, times, out):
                 )
             out_sb = results.tile([P, NT, DH], F32, name="out_sb")
             nc.scalar.copy(out=out_sb[:], in_=bank[:])
-            nc.sync.dma_start(out=out_rows[:, n * NT : (n + 1) * NT, :], in_=out_sb[:])
+            nc.scalar.dma_start(out=out_rows[:, n * NT : (n + 1) * NT, :], in_=out_sb[:])
 
         t_row = const.tile([P, B * L], BF16, name="t_row")
         t_src = const.tile([P, P], BF16, name="t_src")
@@ -159,8 +153,8 @@ def tile_multiscaleretention_pb_kernel(tc, q_rot, k_rot, v, times, out):
         nc.vector.memset(t_flat[:], 0.0)
         nc.vector.memset(ones[:], 1.0)
         nc.scalar.dma_start(out=t_flat[0:1, :], in_=times.rearrange("(o b) l -> o (b l)", o=1))
-        load(0)
-        load(1)
+        for c in range(AHEAD):
+            load(c)
         ident = const.tile([P, P], BF16, name="ident")
         make_identity(nc, ident[:])
 
@@ -221,8 +215,8 @@ def tile_multiscaleretention_pb_kernel(tc, q_rot, k_rot, v, times, out):
         regroup_v(0)
         quantise_v(0)
         for s in range(STEPS + 1):
-            if s % PAIR == 0 and s // PAIR + 2 < STEPS // PAIR:
-                load(s // PAIR + 2)
+            if s % PAIR == 0 and s // PAIR + AHEAD < LOADS:
+                load(s // PAIR + AHEAD)
             if s + 2 < B:
                 prepare_times(s + 2)
             if s + 2 < STEPS:
@@ -236,7 +230,7 @@ def tile_multiscaleretention_pb_kernel(tc, q_rot, k_rot, v, times, out):
                 if i_tile == 0 and s >= 1:
                     quantise(s - 1)
                     product(s - 1)
-            if s % PAIR == 0 and s // PAIR + 1 < STEPS // PAIR:
+            if s % PAIR == 0 and s // PAIR + 1 < LOADS:
                 regroup_v(s // PAIR + 1)
-            if s % PAIR == 1 and s // PAIR + 1 < STEPS // PAIR:
+            if s % PAIR == 1 and s // PAIR + 1 < LOADS:
                 quantise_v(s // PAIR + 1)

import math
from contextlib import ExitStack

import concourse.mybir as mybir
from concourse.masks import make_identity

F32 = mybir.dt.float32
BF16 = mybir.dt.bfloat16
U32 = mybir.dt.uint32
U8 = mybir.dt.uint8
FP8X4 = mybir.dt.float8_e4m3fn_x4
ALU = mybir.AluOpType
ACT = mybir.ActivationFunctionType

H, B, L, DH = 8, 4, 512, 128
P = 128
NT = L // P
STEPS = H * B
PAIR = 2
LOADS = STEPS // PAIR
AHEAD = 5
FAR = 1.0e6
LOG_GAMMA = [math.log(1.0 - 2.0 ** (-5 - h)) for h in range(H)]

FLOPS = 2 * (2 * H * B * L * L * DH)


def tile_multiscaleretention_pb_kernel(tc, q_rot, k_rot, v, times, out):
    nc = tc.nc
    q_rows = q_rot.flatten_outer_dims().rearrange("(g p) d -> p g d", p=P)
    k_rows = k_rot.flatten_outer_dims().rearrange("(g p) d -> p g d", p=P)
    v_rows = v.flatten_outer_dims().rearrange("(g p) d -> p g d", p=P)
    out_rows = out.flatten_outer_dims().rearrange("(g p) d -> p g d", p=P)

    with ExitStack() as stack:
        stack.enter_context(tc.manual_schedule())
        const = stack.enter_context(tc.tile_pool(name="const", bufs=1))
        small = stack.enter_context(tc.tile_pool(name="small", bufs=2))
        loads = stack.enter_context(tc.tile_pool(name="loads", bufs=AHEAD + 1))
        turned = stack.enter_context(tc.tile_pool(name="turned", bufs=3))
        weighed = stack.enter_context(tc.tile_pool(name="weighed", bufs=2))
        values = stack.enter_context(tc.tile_pool(name="values", bufs=3))
        results = stack.enter_context(tc.tile_pool(name="results", bufs=3))
        turn_psum = stack.enter_context(tc.psum_pool(name="turn_psum", bufs=2))
        score_psum = stack.enter_context(tc.psum_pool(name="score_psum", bufs=NT))
        out_psum = stack.enter_context(tc.psum_pool(name="out_psum", bufs=2))

        q_sb, k_sb, v_sb = {}, {}, {}
        v_codes, v_scales, v_grouped = {}, {}, {}
        qk_t, scores, ret_bf, ret_codes, ret_scales = {}, {}, {}, {}, {}

        def load(c):
            slots = slice(c * PAIR * NT, (c + 1) * PAIR * NT)
            q_sb[c] = loads.tile([P, PAIR * NT, DH], BF16, name="q_sb")
            k_sb[c] = loads.tile([P, PAIR * NT, DH], BF16, name="k_sb")
            v_sb[c] = loads.tile([P, PAIR, NT, DH], BF16, name="v_sb")
            nc.sync.dma_start(out=q_sb[c][:], in_=q_rows[:, slots, :])
            nc.sync.dma_start(out=k_sb[c][:], in_=k_rows[:, slots, :])
            nc.sync.dma_start(
                out=v_sb[c][:].rearrange("p b t d -> p (b t) d"), in_=v_rows[:, slots, :]
            )

        def regroup_v(c):
            v_grouped[c] = values.tile([P, PAIR, DH, NT], BF16, name="v_grouped", align_bytes=64)
            nc.scalar.copy(out=v_grouped[c][:], in_=v_sb[c][:].rearrange("p b t d -> p b d t"))

        def quantise_v(c):
            v_codes[c] = values.tile([P, PAIR, DH], U32, name="v_codes", align_bytes=64)
            v_scales[c] = values.tile([P, PAIR, DH], U8, name="v_scales", align_bytes=64)
            nc.vector.quantize_mx(
                out=v_codes[c][:].rearrange("p b d -> p (b d)").bitcast(FP8X4),
                scales=v_scales[c][:].rearrange("p b d -> p (b d)"),
                in_=v_grouped[c][:].rearrange("p b d t -> p (b d t)"),
            )

        def turn(n):
            c, first = n // PAIR, (n % PAIR) * NT
            bank = turn_psum.tile([P, 2 * NT, P], BF16, name="turn_bank")
            for a in range(NT):
                nc.tensor.transpose(out=bank[:, a, :], in_=q_sb[c][:, first + a, :], identity=ident[:])
            for a in range(NT):
                nc.tensor.transpose(
                    out=bank[:, NT + a, :], in_=k_sb[c][:, first + a, :], identity=ident[:]
                )
            qk_t[n] = turned.tile([P, 2 * NT, P], BF16, name="qk_t")
            nc.scalar.copy(out=qk_t[n][:], in_=bank[:])

        def decay_of(n):
            h, b = divmod(n, B)
            for i_tile in range(NT):
                nc.scalar.activation(
                    out=decay[b][:, i_tile, 0 : i_tile + 1, :],
                    in_=delta[b][:, i_tile, 0 : i_tile + 1, :],
                    func=ACT.Exp,
                    scale=LOG_GAMMA[h],
                )

        def score(n, i_tile):
            scores[n, i_tile] = score_psum.tile([P, NT, P], F32, name="score_bank")
            for t in range(NT):
                nc.tensor.matmul(
                    out=scores[n, i_tile][:, t, :],
                    lhsT=qk_t[n][:, NT + t, :],
                    rhs=qk_t[n][:, i_tile, :],
                    start=True,
                    stop=True,
                )

        def weigh(n, i_tile):
            b = n % B
            if i_tile == 0:
                ret_bf[n] = weighed.tile([P, NT, P, NT], BF16, name="ret_bf", align_bytes=64)
            nc.vector.tensor_tensor(
                out=ret_bf[n][:, i_tile, :, :],
                in0=scores[n, i_tile][:].rearrange("p t i -> p i t"),
                in1=decay[b][:, i_tile, :, :].rearrange("p t i -> p i t"),
                op=ALU.mult,
            )

        def quantise(n):
            ret_codes[n] = weighed.tile([P, L], U32, name="ret_codes", align_bytes=64)
            ret_scales[n] = weighed.tile([P, L], U8, name="ret_scales", align_bytes=64)
            nc.vector.quantize_mx(
                out=ret_codes[n][:].bitcast(FP8X4),
                scales=ret_scales[n][:],
                in_=ret_bf[n][:].rearrange("p a i t -> p (a i t)"),
            )

        def product(n):
            c, half = n // PAIR, n % PAIR
            bank = out_psum.tile([P, NT, DH], F32, name="out_bank")
            for i_tile in range(NT):
                cols = slice(i_tile * P, (i_tile + 1) * P)
                nc.tensor.matmul_mx(
                    out=bank[:, i_tile, :],
                    lhsT=ret_codes[n][:, cols].bitcast(FP8X4),
                    lhsT_scale=ret_scales[n][:, cols],
                    rhs=v_codes[c][:, half, :].bitcast(FP8X4),
                    rhs_scale=v_scales[c][:, half, :],
                    start=True,
                    stop=True,
                )
            out_sb = results.tile([P, NT, DH], F32, name="out_sb")
            nc.scalar.copy(out=out_sb[:], in_=bank[:])
            nc.scalar.dma_start(out=out_rows[:, n * NT : (n + 1) * NT, :], in_=out_sb[:])

        t_row = const.tile([P, B * L], BF16, name="t_row")
        t_src = const.tile([P, P], BF16, name="t_src")
        nc.vector.memset(t_src[:], 0.0)
        nc.scalar.dma_start(out=t_src[0 : B * NT, :], in_=times.rearrange("b (t p) -> (b t) p", p=P))
        t_flat = const.tile([P, B * L], BF16, name="t_flat")
        ones = const.tile([P, P], BF16, name="ones")
        nc.vector.memset(t_flat[:], 0.0)
        nc.vector.memset(ones[:], 1.0)
        nc.scalar.dma_start(out=t_flat[0:1, :], in_=times.rearrange("(o b) l -> o (b l)", o=1))
        for c in range(AHEAD):
            load(c)
        ident = const.tile([P, P], BF16, name="ident")
        make_identity(nc, ident[:])

        t_bank = turn_psum.tile([P, 2 * NT, P], BF16, name="turn_bank")
        nc.tensor.transpose(out=t_bank[:, 0, :], in_=t_src[:], identity=ident[:])
        t_key = const.tile([P, B * NT], F32, name="t_key")
        minus_t_key = const.tile([P, B * NT], F32, name="minus_t_key")
        nc.vector.tensor_copy(out=t_key[:], in_=t_bank[:, 0, 0 : B * NT])
        nc.vector.tensor_scalar_mul(out=minus_t_key[:], in0=t_key[:], scalar1=-1.0)
        for b in range(B):
            row_bank = score_psum.tile([P, NT, P], F32, name="score_bank")
            nc.tensor.matmul(
                out=row_bank[:].rearrange("p a i -> p (a i)"),
                lhsT=ones[:],
                rhs=t_flat[:, b * L : (b + 1) * L],
                start=True,
                stop=True,
            )
            nc.scalar.copy(
                out=t_row[:, b * L : (b + 1) * L], in_=row_bank[:].rearrange("p a i -> p (a i)")
            )

        delta = [const.tile([P, NT, NT, P], F32, name="delta%d" % b) for b in range(B)]
        decay = [const.tile([P, NT, NT, P], F32, name="decay%d" % b) for b in range(B)]

        def prepare_times(b):
            row = t_row[:, b * L : (b + 1) * L].rearrange("p (a i) -> p a i", i=P)
            for t in range(NT):
                key_time = t_key[:, b * NT + t : b * NT + t + 1]
                dead = small.tile([P, P], F32, name="dead")
                nc.vector.tensor_scalar(
                    out=dead[:], in0=row[:, t, :], scalar1=key_time, scalar2=FAR,
                    op0=ALU.is_lt, op1=ALU.mult,
                )
                nc.vector.scalar_tensor_tensor(
                    out=delta[b][:, t, t, :], in0=row[:, t, :], scalar=key_time, in1=dead[:],
                    op0=ALU.subtract, op1=ALU.max,
                )
                if t + 1 < NT:
                    nc.scalar.activation(
                        out=delta[b][:, t + 1 : NT, t, :], in_=row[:, t + 1 : NT, :],
                        func=ACT.Identity, bias=minus_t_key[:, b * NT + t : b * NT + t + 1], scale=1.0,
                    )
                if t > 0:
                    nc.vector.tensor_scalar(
                        out=decay[b][:, 0:t, t, :], in0=row[:, 0:t, :], scalar1=key_time, scalar2=None,
                        op0=ALU.is_ge,
                    )

        turn(0)
        prepare_times(0)
        decay_of(0)
        for i_tile in range(NT):
            score(0, i_tile)
        turn(1)
        prepare_times(1)
        decay_of(1)
        regroup_v(0)
        quantise_v(0)
        for s in range(STEPS + 1):
            if s % PAIR == 0 and s // PAIR + AHEAD < LOADS:
                load(s // PAIR + AHEAD)
            if s + 2 < B:
                prepare_times(s + 2)
            if s + 2 < STEPS:
                decay_of(s + 2)
                turn(s + 2)
            for i_tile in range(NT):
                if s < STEPS:
                    weigh(s, i_tile)
                if s + 1 < STEPS:
                    score(s + 1, i_tile)
                if i_tile == 0 and s >= 1:
                    quantise(s - 1)
                    product(s - 1)
            if s % PAIR == 0 and s // PAIR + 1 < LOADS:
                regroup_v(s // PAIR + 1)
            if s % PAIR == 1 and s // PAIR + 1 < LOADS:
                quantise_v(s // PAIR + 1)
